import numpy as np
import ml_dtypes

BF16 = ml_dtypes.bfloat16


def bf(x):
    return np.asarray(x, np.float32).astype(BF16)


def f32(x):
    return np.asarray(x, np.float32)


def f64(x):
    return np.asarray(x).astype(np.float64)


def striped(idx):
    return np.tile(idx.reshape(-1, 16).T, (8, 1))


D, S, N = 128, 1024, 1024


def setup_inputs():
    return {
        "hidden": bf(np.random.standard_normal((D, S))),
        "wq": bf(np.random.standard_normal((D, D)) / np.sqrt(D)),
        "bq": f32(0.1 * np.random.standard_normal((D, 1))),
        "mem": bf(np.random.standard_normal((D, D)) / np.sqrt(D)),
        "z": bf((1.0 + 2.0 * np.random.random((D, 1))) / D),
        "beta": f32(0.5 + np.random.random((1,))),
        "offs": striped(np.random.permutation(np.tile(np.arange(S), 2))[:N]),
    }


def reference(hidden, wq, bq, mem, z, beta, offs):
    idx = offs[:16].T.reshape(-1)
    q = f64(wq).T @ f64(hidden)[:, idx] + f64(bq)
    sq = np.maximum(q, 0.0) + np.exp(np.minimum(q, 0.0))
    num = f64(mem).T @ sq
    den = f64(z).T @ sq
    mix = 1.0 / (1.0 + np.exp(-f64(beta)[0]))
    return mix * num / den + (1.0 - mix) * q

@@ -1,0 +1,113 @@
+import concourse.mybir as mybir
+from concourse.masks import make_identity
+
+F32 = mybir.dt.float32
+BF16 = mybir.dt.bfloat16
+U16 = mybir.dt.uint16
+ALU = mybir.AluOpType
+ACT = mybir.ActivationFunctionType
+
+P = 128
+STORE = 1024
+N = 1024
+PIECE = 512
+BLOCK = 128
+PIECES = N // PIECE
+BLOCKS = PIECE // BLOCK
+
+FLOPS = 2 * P * P * N + 2 * P * P * N + 2 * P * N
+
+
+def tile_infiniattention_kernel(tc, hidden, wq, bq, mem, z, beta, offs, out):
+    nc = tc.nc
+    with (
+        tc.tile_pool(name="held", bufs=1) as held,
+        tc.tile_pool(name="work", bufs=PIECES) as work,
+        tc.psum_pool(name="wide", bufs=2) as wide,
+        tc.psum_pool(name="turned", bufs=2) as turned,
+    ):
+        offsets = held.tile([P, N // 16], U16, name="offsets")
+        nc.sync.dma_start(offsets[:], offs)
+        hidden_sb = held.tile([P, STORE], BF16)
+        nc.sync.dma_start(hidden_sb[:], hidden)
+        wq_sb = held.tile([P, P], BF16)
+        nc.scalar.dma_start(wq_sb[:], wq)
+        mem_sb = held.tile([P, P], BF16)
+        nc.gpsimd.dma_start(mem_sb[:], mem)
+        bq_sb = held.tile([P, 1], F32)
+        z_sb = held.tile([P, 1], BF16)
+        beta_sb = held.tile([P, 1], F32)
+        with nc.allow_non_contiguous_dma(reason="one element to a partition"):
+            nc.scalar.dma_start(bq_sb[:], bq)
+            nc.scalar.dma_start(beta_sb[:], beta.partition_broadcast(P))
+            nc.gpsimd.dma_start(z_sb[:], z)
+        ident = held.tile([P, P], F32)
+        make_identity(nc, ident[:])
+
+        exp_neg_beta = held.tile([P, 1], F32)
+        nc.scalar.activation(exp_neg_beta[:], beta_sb[:], ACT.Exp, scale=-1.0)
+        inv_mix = held.tile([P, 1], F32)
+        nc.vector.tensor_scalar_add(inv_mix[:], exp_neg_beta[:], 1.0)
+        mix = held.tile([P, 1], F32)
+        nc.vector.reciprocal(mix[:], inv_mix[:])
+        rest = held.tile([P, 1], F32)
+        nc.vector.tensor_scalar(rest[:], mix[:], -1.0, 1.0, op0=ALU.mult, op1=ALU.add)
+        neg_rest = held.tile([P, 1], F32)
+        nc.vector.tensor_scalar_add(neg_rest[:], mix[:], -1.0)
+        bq_plus1 = held.tile([P, 1], F32)
+        nc.vector.tensor_scalar_add(bq_plus1[:], bq_sb[:], 1.0)
+
+        q_plus1 = []
+        sq = []
+        for p in range(PIECES):
+            q_ps = wide.tile([P, PIECE], F32, tag="wide")
+            picked = hidden_sb[:].indirect(offsets[:, p * (PIECE // 16) : (p + 1) * (PIECE // 16)])
+            nc.tensor.matmul(q_ps[:], wq_sb[:], picked, start=True, stop=True)
+            exp_q = work.tile([P, PIECE], F32)
+            nc.scalar.activation(exp_q[:], q_ps[:], ACT.Exp, bias=bq_sb[:])
+            q1 = work.tile([P, PIECE], F32)
+            nc.scalar.activation(q1[:], q_ps[:], ACT.Identity, bias=bq_plus1[:])
+            s = work.tile([P, PIECE], BF16)
+            nc.vector.scalar_tensor_tensor(s[:], exp_q[:], 1.0, q1[:], op0=ALU.min, op1=ALU.max)
+            q_plus1.append(q1)
+            sq.append(s)
+
+        read_t = []
+        for p in range(PIECES):
+            den_ps = turned.tile([P, BLOCKS], F32)
+            for b in range(BLOCKS):
+                nc.tensor.matmul(
+                    den_ps[:, b : b + 1], sq[p][:, b * BLOCK : (b + 1) * BLOCK], z_sb[:], start=True, stop=True
+                )
+            den_by_mix = work.tile([P, BLOCKS], F32)
+            nc.vector.tensor_scalar_mul(den_by_mix[:], den_ps[:], inv_mix[:])
+            share = work.tile([P, BLOCKS], F32)
+            nc.vector.reciprocal(share[:], den_by_mix[:])
+            num_even = turned.tile([P, BLOCKS // 2, BLOCK], F32)
+            num_odd = turned.tile([P, BLOCKS // 2, BLOCK], F32)
+            r = work.tile([P, BLOCKS, BLOCK], F32)
+            for b in range(BLOCKS):
+                num_ps = num_even if b % 2 == 0 else num_odd
+                nc.tensor.matmul(
+                    num_ps[:, b // 2, :], sq[p][:, b * BLOCK : (b + 1) * BLOCK], mem_sb[:], start=True, stop=True
+                )
+            for b in range(BLOCKS):
+                if b % 2 == 0:
+                    nc.scalar.activation(
+                        r[:, b, :], num_even[:, b // 2, :], ACT.Identity, bias=neg_rest[:], scale=share[:, b : b + 1]
+                    )
+                else:
+                    nc.vector.tensor_scalar(
+                        r[:, b, :], num_odd[:, b // 2, :], share[:, b : b + 1], neg_rest[:], op0=ALU.mult, op1=ALU.add
+                    )
+            read_t.append(r)
+
+        for p in range(PIECES):
+            read_ps = wide.tile([P, PIECE], F32, tag="wide")
+            for b in range(BLOCKS):
+                nc.tensor.transpose(read_ps[:, b * BLOCK : (b + 1) * BLOCK], read_t[p][:, b, :], ident[:])
+            out_sb = work.tile([P, PIECE], F32)
+            nc.vector.scalar_tensor_tensor(
+                out_sb[:], q_plus1[p][:], rest[:], read_ps[:], op0=ALU.mult, op1=ALU.add
+            )
+            nc.sync.dma_start(out[:, p * PIECE : (p + 1) * PIECE], out_sb[:])

@@ -29,20 +29,25 @@ def tile_infiniattention_kernel(tc, hidden, wq, bq, mem, z, beta, offs, out):
         offsets = held.tile([P, N // 16], U16, name="offsets")
         nc.sync.dma_start(offsets[:], offs)
         hidden_sb = held.tile([P, STORE], BF16)
-        nc.sync.dma_start(hidden_sb[:], hidden)
+        nc.scalar.dma_start(hidden_sb[:], hidden)
         wq_sb = held.tile([P, P], BF16)
-        nc.scalar.dma_start(wq_sb[:], wq)
+        nc.sync.dma_start(wq_sb[:], wq)
         mem_sb = held.tile([P, P], BF16)
         nc.gpsimd.dma_start(mem_sb[:], mem)
         bq_sb = held.tile([P, 1], F32)
         z_sb = held.tile([P, 1], BF16)
         beta_sb = held.tile([P, 1], F32)
         with nc.allow_non_contiguous_dma(reason="one element to a partition"):
-            nc.scalar.dma_start(bq_sb[:], bq)
-            nc.scalar.dma_start(beta_sb[:], beta.partition_broadcast(P))
+            nc.sync.dma_start(bq_sb[:], bq)
+            nc.sync.dma_start(beta_sb[:], beta.partition_broadcast(P))
             nc.gpsimd.dma_start(z_sb[:], z)
         ident = held.tile([P, P], F32)
         make_identity(nc, ident[:])
+
+        zero = held.tile([P, 1], F32)
+        nc.vector.memset(zero[:], 0.0)
+        exp_zero = held.tile([P, 1], F32)
+        nc.scalar.activation(exp_zero[:], zero[:], ACT.Exp)
 
         exp_neg_beta = held.tile([P, 1], F32)
         nc.scalar.activation(exp_neg_beta[:], beta_sb[:], ACT.Exp, scale=-1.0)

@@ -14,6 +14,7 @@ PIECE = 512
 BLOCK = 128
 PIECES = N // PIECE
 BLOCKS = PIECE // BLOCK
+WARM_MATMULS = 5
 
 FLOPS = 2 * P * P * N + 2 * P * P * N + 2 * P * N
 
@@ -48,6 +49,12 @@ def tile_infiniattention_kernel(tc, hidden, wq, bq, mem, z, beta, offs, out):
         nc.vector.memset(zero[:], 0.0)
         exp_zero = held.tile([P, 1], F32)
         nc.scalar.activation(exp_zero[:], zero[:], ACT.Exp)
+
+        warm_sb = held.tile([P, PIECE], BF16)
+        nc.vector.memset(warm_sb[:], 0.0)
+        warm_ps = wide.tile([P, PIECE], F32, tag="wide")
+        for i in range(WARM_MATMULS):
+            nc.tensor.matmul(warm_ps[:], warm_sb[:, 0:P], warm_sb[:], start=True, stop=True)
 
         exp_neg_beta = held.tile([P, 1], F32)
         nc.scalar.activation(exp_neg_beta[:], beta_sb[:], ACT.Exp, scale=-1.0)

@@ -11,10 +11,12 @@ P = 128
 STORE = 1024
 N = 1024
 PIECE = 512
+STEP = 256
 BLOCK = 128
 PIECES = N // PIECE
-BLOCKS = PIECE // BLOCK
-WARM_MATMULS = 5
+STEPS = N // STEP
+BLOCKS = STEP // BLOCK
+BANK = 512
 
 FLOPS = 2 * P * P * N + 2 * P * P * N + 2 * P * N
 
@@ -23,9 +25,9 @@ def tile_infiniattention_kernel(tc, hidden, wq, bq, mem, z, beta, offs, out):
     nc = tc.nc
     with (
         tc.tile_pool(name="held", bufs=1) as held,
-        tc.tile_pool(name="work", bufs=PIECES) as work,
-        tc.psum_pool(name="wide", bufs=2) as wide,
-        tc.psum_pool(name="turned", bufs=2) as turned,
+        tc.tile_pool(name="work", bufs=STEPS) as work,
+        tc.psum_pool(name="wide", bufs=4) as wide,
+        tc.psum_pool(name="turned", bufs=4) as turned,
     ):
         offsets = held.tile([P, N // 16], U16, name="offsets")
         nc.sync.dma_start(offsets[:], offs)
@@ -33,15 +35,14 @@ def tile_infiniattention_kernel(tc, hidden, wq, bq, mem, z, beta, offs, out):
         nc.scalar.dma_start(hidden_sb[:], hidden)
         wq_sb = held.tile([P, P], BF16)
         nc.sync.dma_start(wq_sb[:], wq)
-        mem_sb = held.tile([P, P], BF16)
-        nc.gpsimd.dma_start(mem_sb[:], mem)
+        mem_z = held.tile([P, P + 1], BF16)
+        nc.gpsimd.dma_start(mem_z[:, 0:P], mem)
         bq_sb = held.tile([P, 1], F32)
-        z_sb = held.tile([P, 1], BF16)
         beta_sb = held.tile([P, 1], F32)
         with nc.allow_non_contiguous_dma(reason="one element to a partition"):
             nc.sync.dma_start(bq_sb[:], bq)
             nc.sync.dma_start(beta_sb[:], beta.partition_broadcast(P))
-            nc.gpsimd.dma_start(z_sb[:], z)
+            nc.gpsimd.dma_start(mem_z[:, P : P + 1], z)
         ident = held.tile([P, P], F32)
         make_identity(nc, ident[:])
 
@@ -49,12 +50,6 @@ def tile_infiniattention_kernel(tc, hidden, wq, bq, mem, z, beta, offs, out):
         nc.vector.memset(zero[:], 0.0)
         exp_zero = held.tile([P, 1], F32)
         nc.scalar.activation(exp_zero[:], zero[:], ACT.Exp)
-
-        warm_sb = held.tile([P, PIECE], BF16)
-        nc.vector.memset(warm_sb[:], 0.0)
-        warm_ps = wide.tile([P, PIECE], F32, tag="wide")
-        for i in range(WARM_MATMULS):
-            nc.tensor.matmul(warm_ps[:], warm_sb[:, 0:P], warm_sb[:], start=True, stop=True)
 
         exp_neg_beta = held.tile([P, 1], F32)
         nc.scalar.activation(exp_neg_beta[:], beta_sb[:], ACT.Exp, scale=-1.0)
@@ -69,57 +64,55 @@ def tile_infiniattention_kernel(tc, hidden, wq, bq, mem, z, beta, offs, out):
         bq_plus1 = held.tile([P, 1], F32)
         nc.vector.tensor_scalar_add(bq_plus1[:], bq_sb[:], 1.0)
 
-        q_plus1 = []
-        sq = []
+        q_banks = []
         for p in range(PIECES):
             q_ps = wide.tile([P, PIECE], F32, tag="wide")
             picked = hidden_sb[:].indirect(offsets[:, p * (PIECE // 16) : (p + 1) * (PIECE // 16)])
             nc.tensor.matmul(q_ps[:], wq_sb[:], picked, start=True, stop=True)
-            exp_q = work.tile([P, PIECE], F32)
-            nc.scalar.activation(exp_q[:], q_ps[:], ACT.Exp, bias=bq_sb[:])
-            q1 = work.tile([P, PIECE], F32)
-            nc.scalar.activation(q1[:], q_ps[:], ACT.Identity, bias=bq_plus1[:])
-            s = work.tile([P, PIECE], BF16)
-            nc.vector.scalar_tensor_tensor(s[:], exp_q[:], 1.0, q1[:], op0=ALU.min, op1=ALU.max)
+            q_banks.append(q_ps)
+
+        q_plus1 = []
+        sq = []
+        for s in range(STEPS):
+            q_step = q_banks[s * STEP // PIECE][:, s * STEP % PIECE : s * STEP % PIECE + STEP]
+            exp_q = work.tile([P, STEP], F32)
+            nc.scalar.activation(exp_q[:], q_step, ACT.Exp, bias=bq_sb[:])
+            q1 = work.tile([P, STEP], F32)
+            nc.scalar.activation(q1[:], q_step, ACT.Identity, bias=bq_plus1[:])
+            sq_step = work.tile([P, STEP], BF16)
+            nc.vector.scalar_tensor_tensor(sq_step[:], exp_q[:], 1.0, q1[:], op0=ALU.min, op1=ALU.max)
             q_plus1.append(q1)
-            sq.append(s)
+            sq.append(sq_step)
 
         read_t = []
-        for p in range(PIECES):
-            den_ps = turned.tile([P, BLOCKS], F32)
+        for s in range(STEPS):
+            num_den = turned.tile([P, BLOCKS, BANK // BLOCKS], F32)
             for b in range(BLOCKS):
                 nc.tensor.matmul(
-                    den_ps[:, b : b + 1], sq[p][:, b * BLOCK : (b + 1) * BLOCK], z_sb[:], start=True, stop=True
+                    num_den[:, b, 0 : P + 1], sq[s][:, b * BLOCK : (b + 1) * BLOCK], mem_z[:], start=True, stop=True
                 )
-            den_by_mix = work.tile([P, BLOCKS], F32)
-            nc.vector.tensor_scalar_mul(den_by_mix[:], den_ps[:], inv_mix[:])
-            share = work.tile([P, BLOCKS], F32)
+            den_by_mix = work.tile([P, BLOCKS, 1], F32)
+            nc.vector.tensor_scalar_mul(den_by_mix[:], num_den[:, :, P : P + 1], inv_mix[:])
+            share = work.tile([P, BLOCKS, 1], F32)
             nc.vector.reciprocal(share[:], den_by_mix[:])
-            num_even = turned.tile([P, BLOCKS // 2, BLOCK], F32)
-            num_odd = turned.tile([P, BLOCKS // 2, BLOCK], F32)
             r = work.tile([P, BLOCKS, BLOCK], F32)
             for b in range(BLOCKS):
-                num_ps = num_even if b % 2 == 0 else num_odd
-                nc.tensor.matmul(
-                    num_ps[:, b // 2, :], sq[p][:, b * BLOCK : (b + 1) * BLOCK], mem_sb[:], start=True, stop=True
-                )
-            for b in range(BLOCKS):
-                if b % 2 == 0:
-                    nc.scalar.activation(
-                        r[:, b, :], num_even[:, b // 2, :], ACT.Identity, bias=neg_rest[:], scale=share[:, b : b + 1]
+                if s < STEPS // 2:
+                    nc.vector.tensor_scalar(
+                        r[:, b, :], num_den[:, b, 0:P], share[:, b, :], neg_rest[:], op0=ALU.mult, op1=ALU.add
                     )
                 else:
-                    nc.vector.tensor_scalar(
-                        r[:, b, :], num_odd[:, b // 2, :], share[:, b : b + 1], neg_rest[:], op0=ALU.mult, op1=ALU.add
+                    nc.scalar.activation(
+                        r[:, b, :], num_den[:, b, 0:P], ACT.Identity, bias=neg_rest[:], scale=share[:, b, :]
                     )
             read_t.append(r)
 
-        for p in range(PIECES):
-            read_ps = wide.tile([P, PIECE], F32, tag="wide")
+        for s in range(STEPS):
+            read_ps = wide.tile([P, STEP], F32, tag="wide")
             for b in range(BLOCKS):
-                nc.tensor.transpose(read_ps[:, b * BLOCK : (b + 1) * BLOCK], read_t[p][:, b, :], ident[:])
-            out_sb = work.tile([P, PIECE], F32)
+                nc.tensor.transpose(read_ps[:, b * BLOCK : (b + 1) * BLOCK], read_t[s][:, b, :], ident[:])
+            out_sb = work.tile([P, STEP], F32)
             nc.vector.scalar_tensor_tensor(
-                out_sb[:], q_plus1[p][:], rest[:], read_ps[:], op0=ALU.mult, op1=ALU.add
+                out_sb[:], q_plus1[s][:], rest[:], read_ps[:], op0=ALU.mult, op1=ALU.add
             )
-            nc.sync.dma_start(out[:, p * PIECE : (p + 1) * PIECE], out_sb[:])
+            nc.sync.dma_start(out[:, s * STEP : (s + 1) * STEP], out_sb[:])

@@ -11,12 +11,16 @@ P = 128
 STORE = 1024
 N = 1024
 PIECE = 512
-STEP = 256
-BLOCK = 128
 PIECES = N // PIECE
-STEPS = N // STEP
-BLOCKS = STEP // BLOCK
+BLOCK = 128
+STEP_WIDTHS = (256, 256, 256, 128, 128)
+STEPS = len(STEP_WIDTHS)
+STEP_STARTS = tuple(sum(STEP_WIDTHS[:s]) for s in range(STEPS))
+MAX_BLOCKS = max(STEP_WIDTHS) // BLOCK
 BANK = 512
+
+assert sum(STEP_WIDTHS) == N
+assert all(start // PIECE == (start + width - 1) // PIECE for start, width in zip(STEP_STARTS, STEP_WIDTHS))
 
 FLOPS = 2 * P * P * N + 2 * P * P * N + 2 * P * N
 
@@ -36,15 +40,16 @@ def tile_infiniattention_kernel(tc, hidden, wq, bq, mem, z, beta, offs, out):
         wq_sb = held.tile([P, P], BF16)
         nc.sync.dma_start(wq_sb[:], wq)
         mem_z = held.tile([P, P + 1], BF16)
-        nc.gpsimd.dma_start(mem_z[:, 0:P], mem)
+        nc.scalar.dma_start(mem_z[:, 0:P], mem)
         bq_sb = held.tile([P, 1], F32)
         beta_sb = held.tile([P, 1], F32)
         with nc.allow_non_contiguous_dma(reason="one element to a partition"):
             nc.sync.dma_start(bq_sb[:], bq)
             nc.sync.dma_start(beta_sb[:], beta.partition_broadcast(P))
-            nc.gpsimd.dma_start(mem_z[:, P : P + 1], z)
+            nc.scalar.dma_start(mem_z[:, P : P + 1], z)
         ident = held.tile([P, P], F32)
-        make_identity(nc, ident[:])
+        nc.vector.memset(ident[:], 0.0)
+        make_identity(nc, ident[:], nomemset=True)
 
         zero = held.tile([P, 1], F32)
         nc.vector.memset(zero[:], 0.0)
@@ -73,30 +78,31 @@ def tile_infiniattention_kernel(tc, hidden, wq, bq, mem, z, beta, offs, out):
 
         q_plus1 = []
         sq = []
-        for s in range(STEPS):
-            q_step = q_banks[s * STEP // PIECE][:, s * STEP % PIECE : s * STEP % PIECE + STEP]
-            exp_q = work.tile([P, STEP], F32)
+        for start, width in zip(STEP_STARTS, STEP_WIDTHS):
+            q_step = q_banks[start // PIECE][:, start % PIECE : start % PIECE + width]
+            exp_q = work.tile([P, width], F32, tag="exp_q")
             nc.scalar.activation(exp_q[:], q_step, ACT.Exp, bias=bq_sb[:])
-            q1 = work.tile([P, STEP], F32)
+            q1 = work.tile([P, width], F32, tag="q1")
             nc.scalar.activation(q1[:], q_step, ACT.Identity, bias=bq_plus1[:])
-            sq_step = work.tile([P, STEP], BF16)
+            sq_step = work.tile([P, width], BF16, tag="sq_step")
             nc.vector.scalar_tensor_tensor(sq_step[:], exp_q[:], 1.0, q1[:], op0=ALU.min, op1=ALU.max)
             q_plus1.append(q1)
             sq.append(sq_step)
 
         read_t = []
         for s in range(STEPS):
-            num_den = turned.tile([P, BLOCKS, BANK // BLOCKS], F32)
-            for b in range(BLOCKS):
+            blocks = STEP_WIDTHS[s] // BLOCK
+            num_den = turned.tile([P, MAX_BLOCKS, BANK // MAX_BLOCKS], F32)
+            for b in range(blocks):
                 nc.tensor.matmul(
                     num_den[:, b, 0 : P + 1], sq[s][:, b * BLOCK : (b + 1) * BLOCK], mem_z[:], start=True, stop=True
                 )
-            den_by_mix = work.tile([P, BLOCKS, 1], F32)
-            nc.vector.tensor_scalar_mul(den_by_mix[:], num_den[:, :, P : P + 1], inv_mix[:])
-            share = work.tile([P, BLOCKS, 1], F32)
-            nc.vector.reciprocal(share[:], den_by_mix[:])
-            r = work.tile([P, BLOCKS, BLOCK], F32)
-            for b in range(BLOCKS):
+            den_by_mix = work.tile([P, MAX_BLOCKS, 1], F32)
+            nc.vector.tensor_scalar_mul(den_by_mix[:, 0:blocks, :], num_den[:, 0:blocks, P : P + 1], inv_mix[:])
+            share = work.tile([P, MAX_BLOCKS, 1], F32)
+            nc.vector.reciprocal(share[:, 0:blocks, :], den_by_mix[:, 0:blocks, :])
+            r = work.tile([P, MAX_BLOCKS, BLOCK], F32)
+            for b in range(blocks):
                 if s < STEPS // 2:
                     nc.vector.tensor_scalar(
                         r[:, b, :], num_den[:, b, 0:P], share[:, b, :], neg_rest[:], op0=ALU.mult, op1=ALU.add
@@ -108,11 +114,12 @@ def tile_infiniattention_kernel(tc, hidden, wq, bq, mem, z, beta, offs, out):
             read_t.append(r)
 
         for s in range(STEPS):
-            read_ps = wide.tile([P, STEP], F32, tag="wide")
-            for b in range(BLOCKS):
+            start, width = STEP_STARTS[s], STEP_WIDTHS[s]
+            read_ps = wide.tile([P, width], F32, tag="wide")
+            for b in range(width // BLOCK):
                 nc.tensor.transpose(read_ps[:, b * BLOCK : (b + 1) * BLOCK], read_t[s][:, b, :], ident[:])
-            out_sb = work.tile([P, STEP], F32)
+            out_sb = work.tile([P, width], F32, tag="out_sb")
             nc.vector.scalar_tensor_tensor(
                 out_sb[:], q_plus1[s][:], rest[:], read_ps[:], op0=ALU.mult, op1=ALU.add
             )
-            nc.sync.dma_start(out[:, s * STEP : (s + 1) * STEP], out_sb[:])
+            nc.sync.dma_start(out[:, start : start + width], out_sb[:])

@@ -10,7 +10,7 @@ ACT = mybir.ActivationFunctionType
 P = 128
 STORE = 1024
 N = 1024
-PIECE = 512
+PIECE = 256
 PIECES = N // PIECE
 BLOCK = 128
 STEP_WIDTHS = (256, 256, 256, 128, 128)
@@ -56,6 +56,8 @@ def tile_infiniattention_kernel(tc, hidden, wq, bq, mem, z, beta, offs, out):
         exp_zero = held.tile([P, 1], F32)
         nc.scalar.activation(exp_zero[:], zero[:], ACT.Exp)
 
+        bq_plus1 = held.tile([P, 1], F32)
+        nc.vector.tensor_scalar_add(bq_plus1[:], bq_sb[:], 1.0)
         exp_neg_beta = held.tile([P, 1], F32)
         nc.scalar.activation(exp_neg_beta[:], beta_sb[:], ACT.Exp, scale=-1.0)
         inv_mix = held.tile([P, 1], F32)
@@ -66,8 +68,6 @@ def tile_infiniattention_kernel(tc, hidden, wq, bq, mem, z, beta, offs, out):
         nc.vector.tensor_scalar(rest[:], mix[:], -1.0, 1.0, op0=ALU.mult, op1=ALU.add)
         neg_rest = held.tile([P, 1], F32)
         nc.vector.tensor_scalar_add(neg_rest[:], mix[:], -1.0)
-        bq_plus1 = held.tile([P, 1], F32)
-        nc.vector.tensor_scalar_add(bq_plus1[:], bq_sb[:], 1.0)
 
         q_banks = []
         for p in range(PIECES):

@@ -33,12 +33,13 @@ def tile_infiniattention_kernel(tc, hidden, wq, bq, mem, z, beta, offs, out):
         tc.psum_pool(name="wide", bufs=4) as wide,
         tc.psum_pool(name="turned", bufs=4) as turned,
     ):
+        hidden_sb = held.tile([P, STORE], BF16)
+        nc.scalar.dma_start(hidden_sb[:, 0 : STORE // 2], hidden[:, 0 : STORE // 2])
+        nc.sync.dma_start(hidden_sb[:, STORE // 2 : STORE], hidden[:, STORE // 2 : STORE])
         offsets = held.tile([P, N // 16], U16, name="offsets")
         nc.sync.dma_start(offsets[:], offs)
-        hidden_sb = held.tile([P, STORE], BF16)
-        nc.scalar.dma_start(hidden_sb[:], hidden)
         wq_sb = held.tile([P, P], BF16)
-        nc.sync.dma_start(wq_sb[:], wq)
+        nc.scalar.dma_start(wq_sb[:], wq)
         mem_z = held.tile([P, P + 1], BF16)
         nc.scalar.dma_start(mem_z[:, 0:P], mem)
         bq_sb = held.tile([P, 1], F32)

@@ -10,17 +10,16 @@ ACT = mybir.ActivationFunctionType
 P = 128
 STORE = 1024
 N = 1024
-PIECE = 256
-PIECES = N // PIECE
 BLOCK = 128
 STEP_WIDTHS = (256, 256, 256, 128, 128)
 STEPS = len(STEP_WIDTHS)
 STEP_STARTS = tuple(sum(STEP_WIDTHS[:s]) for s in range(STEPS))
 MAX_BLOCKS = max(STEP_WIDTHS) // BLOCK
 BANK = 512
+PSUM_BANKS = 8
 
 assert sum(STEP_WIDTHS) == N
-assert all(start // PIECE == (start + width - 1) // PIECE for start, width in zip(STEP_STARTS, STEP_WIDTHS))
+assert all(start % 32 == 0 and width % 16 == 0 for start, width in zip(STEP_STARTS, STEP_WIDTHS))
 
 FLOPS = 2 * P * P * N + 2 * P * P * N + 2 * P * N
 
@@ -30,8 +29,7 @@ def tile_infiniattention_kernel(tc, hidden, wq, bq, mem, z, beta, offs, out):
     with (
         tc.tile_pool(name="held", bufs=1) as held,
         tc.tile_pool(name="work", bufs=STEPS) as work,
-        tc.psum_pool(name="wide", bufs=4) as wide,
-        tc.psum_pool(name="turned", bufs=4) as turned,
+        tc.psum_pool(name="banks", bufs=PSUM_BANKS) as banks,
     ):
         hidden_sb = held.tile([P, STORE], BF16)
         nc.scalar.dma_start(hidden_sb[:, 0 : STORE // 2], hidden[:, 0 : STORE // 2])
@@ -67,60 +65,61 @@ def tile_infiniattention_kernel(tc, hidden, wq, bq, mem, z, beta, offs, out):
         nc.vector.reciprocal(mix[:], inv_mix[:])
         rest = held.tile([P, 1], F32)
         nc.vector.tensor_scalar(rest[:], mix[:], -1.0, 1.0, op0=ALU.mult, op1=ALU.add)
-        neg_rest = held.tile([P, 1], F32)
-        nc.vector.tensor_scalar_add(neg_rest[:], mix[:], -1.0)
+        rest_bq = held.tile([P, 1], F32)
+        nc.vector.tensor_mul(rest_bq[:], rest[:], bq_sb[:])
 
-        q_banks = []
-        for p in range(PIECES):
-            q_ps = wide.tile([P, PIECE], F32, tag="wide")
-            picked = hidden_sb[:].indirect(offsets[:, p * (PIECE // 16) : (p + 1) * (PIECE // 16)])
-            nc.tensor.matmul(q_ps[:], wq_sb[:], picked, start=True, stop=True)
-            q_banks.append(q_ps)
-
-        q_plus1 = []
-        sq = []
+        q_ps = []
         for start, width in zip(STEP_STARTS, STEP_WIDTHS):
-            q_step = q_banks[start // PIECE][:, start % PIECE : start % PIECE + width]
-            exp_q = work.tile([P, width], F32, tag="exp_q")
-            nc.scalar.activation(exp_q[:], q_step, ACT.Exp, bias=bq_sb[:])
-            q1 = work.tile([P, width], F32, tag="q1")
-            nc.scalar.activation(q1[:], q_step, ACT.Identity, bias=bq_plus1[:])
+            q_step = banks.tile([P, BANK], F32, tag="bank")
+            picked = hidden_sb[:].indirect(offsets[:, start // 16 : (start + width) // 16])
+            nc.tensor.matmul(q_step[:, 0:width], wq_sb[:], picked, start=True, stop=True)
+            q_ps.append(q_step)
+
+        sq = []
+        for s in range(STEPS):
+            width = STEP_WIDTHS[s]
+            exp_q = work.tile([P, width], BF16, tag="exp_q")
+            nc.scalar.activation(exp_q[:], q_ps[s][:, 0:width], ACT.Exp, bias=bq_sb[:])
+            exp_cut = work.tile([P, width], BF16, tag="exp_cut")
+            nc.vector.tensor_scalar_min(exp_cut[:], exp_q[:], 1.0)
             sq_step = work.tile([P, width], BF16, tag="sq_step")
-            nc.vector.scalar_tensor_tensor(sq_step[:], exp_q[:], 1.0, q1[:], op0=ALU.min, op1=ALU.max)
-            q_plus1.append(q1)
+            nc.vector.scalar_tensor_tensor(
+                sq_step[:], q_ps[s][:, 0:width], bq_plus1[:], exp_cut[:], op0=ALU.add, op1=ALU.max
+            )
             sq.append(sq_step)
+
+        q_share = []
+        for s in range(STEPS):
+            width = STEP_WIDTHS[s]
+            share_step = work.tile([P, width], F32, tag="share_step")
+            nc.scalar.activation(share_step[:], q_ps[s][:, 0:width], ACT.Identity, bias=rest_bq[:], scale=rest[:])
+            q_share.append(share_step)
 
         read_t = []
         for s in range(STEPS):
             blocks = STEP_WIDTHS[s] // BLOCK
-            num_den = turned.tile([P, MAX_BLOCKS, BANK // MAX_BLOCKS], F32)
+            num_den = banks.tile([P, MAX_BLOCKS, BANK // MAX_BLOCKS], F32, tag="bank")
             for b in range(blocks):
                 nc.tensor.matmul(
                     num_den[:, b, 0 : P + 1], sq[s][:, b * BLOCK : (b + 1) * BLOCK], mem_z[:], start=True, stop=True
                 )
-            den_by_mix = work.tile([P, MAX_BLOCKS, 1], F32)
-            nc.vector.tensor_scalar_mul(den_by_mix[:, 0:blocks, :], num_den[:, 0:blocks, P : P + 1], inv_mix[:])
-            share = work.tile([P, MAX_BLOCKS, 1], F32)
-            nc.vector.reciprocal(share[:, 0:blocks, :], den_by_mix[:, 0:blocks, :])
+            inv_den = work.tile([P, MAX_BLOCKS, 1], F32)
+            nc.vector.reciprocal(inv_den[:, 0:blocks, :], num_den[:, 0:blocks, P : P + 1])
             r = work.tile([P, MAX_BLOCKS, BLOCK], F32)
             for b in range(blocks):
                 if s < STEPS // 2:
-                    nc.vector.tensor_scalar(
-                        r[:, b, :], num_den[:, b, 0:P], share[:, b, :], neg_rest[:], op0=ALU.mult, op1=ALU.add
-                    )
+                    nc.vector.tensor_scalar_mul(r[:, b, :], num_den[:, b, 0:P], inv_den[:, b, :])
                 else:
-                    nc.scalar.activation(
-                        r[:, b, :], num_den[:, b, 0:P], ACT.Identity, bias=neg_rest[:], scale=share[:, b, :]
-                    )
+                    nc.scalar.activation(r[:, b, :], num_den[:, b, 0:P], ACT.Identity, scale=inv_den[:, b, :])
             read_t.append(r)
 
         for s in range(STEPS):
             start, width = STEP_STARTS[s], STEP_WIDTHS[s]
-            read_ps = wide.tile([P, width], F32, tag="wide")
+            read_ps = banks.tile([P, BANK], F32, tag="bank")
             for b in range(width // BLOCK):
                 nc.tensor.transpose(read_ps[:, b * BLOCK : (b + 1) * BLOCK], read_t[s][:, b, :], ident[:])
             out_sb = work.tile([P, width], F32, tag="out_sb")
             nc.vector.scalar_tensor_tensor(
-                out_sb[:], q_plus1[s][:], rest[:], read_ps[:], op0=ALU.mult, op1=ALU.add
+                out_sb[:], read_ps[:, 0:width], mix[:], q_share[s][:], op0=ALU.mult, op1=ALU.add
             )
             nc.sync.dma_start(out[:, start : start + width], out_sb[:])

@@ -11,7 +11,7 @@ P = 128
 STORE = 1024
 N = 1024
 BLOCK = 128
-STEP_WIDTHS = (256, 256, 256, 128, 128)
+STEP_WIDTHS = (128, 256, 256, 256, 128)
 STEPS = len(STEP_WIDTHS)
 STEP_STARTS = tuple(sum(STEP_WIDTHS[:s]) for s in range(STEPS))
 MAX_BLOCKS = max(STEP_WIDTHS) // BLOCK

@@ -32,20 +32,20 @@ def tile_infiniattention_kernel(tc, hidden, wq, bq, mem, z, beta, offs, out):
         tc.psum_pool(name="banks", bufs=PSUM_BANKS) as banks,
     ):
         hidden_sb = held.tile([P, STORE], BF16)
-        nc.scalar.dma_start(hidden_sb[:, 0 : STORE // 2], hidden[:, 0 : STORE // 2])
-        nc.sync.dma_start(hidden_sb[:, STORE // 2 : STORE], hidden[:, STORE // 2 : STORE])
+        for half in (slice(0, STORE // 2), slice(STORE // 2, STORE)):
+            nc.sync.dma_start(hidden_sb[:, half], hidden[:, half])
         offsets = held.tile([P, N // 16], U16, name="offsets")
         nc.sync.dma_start(offsets[:], offs)
         wq_sb = held.tile([P, P], BF16)
-        nc.scalar.dma_start(wq_sb[:], wq)
-        mem_z = held.tile([P, P + 1], BF16)
-        nc.scalar.dma_start(mem_z[:, 0:P], mem)
+        nc.sync.dma_start(wq_sb[:], wq)
         bq_sb = held.tile([P, 1], F32)
         beta_sb = held.tile([P, 1], F32)
+        mem_z = held.tile([P, P + 1], BF16)
         with nc.allow_non_contiguous_dma(reason="one element to a partition"):
             nc.sync.dma_start(bq_sb[:], bq)
             nc.sync.dma_start(beta_sb[:], beta.partition_broadcast(P))
-            nc.scalar.dma_start(mem_z[:, P : P + 1], z)
+            nc.sync.dma_start(mem_z[:, 0:P], mem)
+            nc.sync.dma_start(mem_z[:, P : P + 1], z)
         ident = held.tile([P, P], F32)
         nc.vector.memset(ident[:], 0.0)
         make_identity(nc, ident[:], nomemset=True)

@@ -57,16 +57,18 @@ def tile_infiniattention_kernel(tc, hidden, wq, bq, mem, z, beta, offs, out):
 
         bq_plus1 = held.tile([P, 1], F32)
         nc.vector.tensor_scalar_add(bq_plus1[:], bq_sb[:], 1.0)
-        exp_neg_beta = held.tile([P, 1], F32)
-        nc.scalar.activation(exp_neg_beta[:], beta_sb[:], ACT.Exp, scale=-1.0)
-        inv_mix = held.tile([P, 1], F32)
-        nc.vector.tensor_scalar_add(inv_mix[:], exp_neg_beta[:], 1.0)
-        mix = held.tile([P, 1], F32)
-        nc.vector.reciprocal(mix[:], inv_mix[:])
+        half_bq = held.tile([P, 1], F32)
+        nc.vector.tensor_scalar_mul(half_bq[:], bq_sb[:], 0.5)
+        minus_half_bq = held.tile([P, 1], F32)
+        nc.vector.tensor_scalar_mul(minus_half_bq[:], bq_sb[:], -0.5)
+        tanh_half = held.tile([P, 1], F32)
+        nc.scalar.activation(tanh_half[:], beta_sb[:], ACT.Tanh, scale=0.5)
         rest = held.tile([P, 1], F32)
-        nc.vector.tensor_scalar(rest[:], mix[:], -1.0, 1.0, op0=ALU.mult, op1=ALU.add)
+        nc.vector.tensor_scalar(rest[:], tanh_half[:], -0.5, 0.5, op0=ALU.mult, op1=ALU.add)
         rest_bq = held.tile([P, 1], F32)
-        nc.vector.tensor_mul(rest_bq[:], rest[:], bq_sb[:])
+        nc.vector.tensor_scalar(rest_bq[:], tanh_half[:], minus_half_bq[:], half_bq[:], op0=ALU.mult, op1=ALU.add)
+        mix = held.tile([P, 1], F32)
+        nc.vector.tensor_scalar(mix[:], tanh_half[:], 0.5, 0.5, op0=ALU.mult, op1=ALU.add)
 
         q_ps = []
         for start, width in zip(STEP_STARTS, STEP_WIDTHS):

@@ -15,6 +15,7 @@ STEP_WIDTHS = (128, 256, 256, 256, 128)
 STEPS = len(STEP_WIDTHS)
 STEP_STARTS = tuple(sum(STEP_WIDTHS[:s]) for s in range(STEPS))
 MAX_BLOCKS = max(STEP_WIDTHS) // BLOCK
+LAG = 2
 BANK = 512
 PSUM_BANKS = 8
 
@@ -78,17 +79,43 @@ def tile_infiniattention_kernel(tc, hidden, wq, bq, mem, z, beta, offs, out):
             q_ps.append(q_step)
 
         sq = []
-        for s in range(STEPS):
-            width = STEP_WIDTHS[s]
-            exp_q = work.tile([P, width], BF16, tag="exp_q")
-            nc.scalar.activation(exp_q[:], q_ps[s][:, 0:width], ACT.Exp, bias=bq_sb[:])
-            exp_cut = work.tile([P, width], BF16, tag="exp_cut")
-            nc.vector.tensor_scalar_min(exp_cut[:], exp_q[:], 1.0)
-            sq_step = work.tile([P, width], BF16, tag="sq_step")
-            nc.vector.scalar_tensor_tensor(
-                sq_step[:], q_ps[s][:, 0:width], bq_plus1[:], exp_cut[:], op0=ALU.add, op1=ALU.max
-            )
-            sq.append(sq_step)
+        num_den_ps = []
+        inv_dens = []
+        read_t = []
+        for t in range(STEPS + 2 * LAG):
+            if t < STEPS:
+                width = STEP_WIDTHS[t]
+                exp_q = work.tile([P, width], BF16, tag="exp_q")
+                nc.scalar.activation(exp_q[:], q_ps[t][:, 0:width], ACT.Exp, bias=bq_sb[:])
+                exp_cut = work.tile([P, width], BF16, tag="exp_cut")
+                nc.vector.tensor_scalar_min(exp_cut[:], exp_q[:], 1.0)
+                sq_step = work.tile([P, width], BF16, tag="sq_step")
+                nc.vector.scalar_tensor_tensor(
+                    sq_step[:], q_ps[t][:, 0:width], bq_plus1[:], exp_cut[:], op0=ALU.add, op1=ALU.max
+                )
+                sq.append(sq_step)
+            s = t - LAG
+            if 0 <= s < STEPS:
+                blocks = STEP_WIDTHS[s] // BLOCK
+                num_den = banks.tile([P, MAX_BLOCKS, BANK // MAX_BLOCKS], F32, tag="bank")
+                for b in range(blocks):
+                    nc.tensor.matmul(
+                        num_den[:, b, 0 : P + 1], sq[s][:, b * BLOCK : (b + 1) * BLOCK], mem_z[:], start=True, stop=True
+                    )
+                inv_den = work.tile([P, MAX_BLOCKS, 1], F32)
+                nc.vector.reciprocal(inv_den[:, 0:blocks, :], num_den[:, 0:blocks, P : P + 1])
+                num_den_ps.append(num_den)
+                inv_dens.append(inv_den)
+            s = t - 2 * LAG
+            if s >= 0:
+                r = work.tile([P, MAX_BLOCKS, BLOCK], F32)
+                for b in range(STEP_WIDTHS[s] // BLOCK):
+                    num, factor = num_den_ps[s][:, b, 0:P], inv_dens[s][:, b, :]
+                    if s < STEPS // 2:
+                        nc.vector.tensor_scalar_mul(r[:, b, :], num, factor)
+                    else:
+                        nc.scalar.activation(r[:, b, :], num, ACT.Identity, scale=factor)
+                read_t.append(r)
 
         q_share = []
         for s in range(STEPS):
@@ -96,24 +123,6 @@ def tile_infiniattention_kernel(tc, hidden, wq, bq, mem, z, beta, offs, out):
             share_step = work.tile([P, width], F32, tag="share_step")
             nc.scalar.activation(share_step[:], q_ps[s][:, 0:width], ACT.Identity, bias=rest_bq[:], scale=rest[:])
             q_share.append(share_step)
-
-        read_t = []
-        for s in range(STEPS):
-            blocks = STEP_WIDTHS[s] // BLOCK
-            num_den = banks.tile([P, MAX_BLOCKS, BANK // MAX_BLOCKS], F32, tag="bank")
-            for b in range(blocks):
-                nc.tensor.matmul(
-                    num_den[:, b, 0 : P + 1], sq[s][:, b * BLOCK : (b + 1) * BLOCK], mem_z[:], start=True, stop=True
-                )
-            inv_den = work.tile([P, MAX_BLOCKS, 1], F32)
-            nc.vector.reciprocal(inv_den[:, 0:blocks, :], num_den[:, 0:blocks, P : P + 1])
-            r = work.tile([P, MAX_BLOCKS, BLOCK], F32)
-            for b in range(blocks):
-                if s < STEPS // 2:
-                    nc.vector.tensor_scalar_mul(r[:, b, :], num_den[:, b, 0:P], inv_den[:, b, :])
-                else:
-                    nc.scalar.activation(r[:, b, :], num_den[:, b, 0:P], ACT.Identity, scale=inv_den[:, b, :])
-            read_t.append(r)
 
         for s in range(STEPS):
             start, width = STEP_STARTS[s], STEP_WIDTHS[s]

import concourse.mybir as mybir
from concourse.masks import make_identity

F32 = mybir.dt.float32
BF16 = mybir.dt.bfloat16
U16 = mybir.dt.uint16
ALU = mybir.AluOpType
ACT = mybir.ActivationFunctionType

P = 128
STORE = 1024
N = 1024
BLOCK = 128
STEP_WIDTHS = (128, 256, 256, 256, 128)
STEPS = len(STEP_WIDTHS)
STEP_STARTS = tuple(sum(STEP_WIDTHS[:s]) for s in range(STEPS))
MAX_BLOCKS = max(STEP_WIDTHS) // BLOCK
LAG = 2
BANK = 512
PSUM_BANKS = 8

assert sum(STEP_WIDTHS) == N
assert all(start % 32 == 0 and width % 16 == 0 for start, width in zip(STEP_STARTS, STEP_WIDTHS))

FLOPS = 2 * P * P * N + 2 * P * P * N + 2 * P * N


def tile_infiniattention_kernel(tc, hidden, wq, bq, mem, z, beta, offs, out):
    nc = tc.nc
    with (
        tc.tile_pool(name="held", bufs=1) as held,
        tc.tile_pool(name="work", bufs=STEPS) as work,
        tc.psum_pool(name="banks", bufs=PSUM_BANKS) as banks,
    ):
        hidden_sb = held.tile([P, STORE], BF16)
        for half in (slice(0, STORE // 2), slice(STORE // 2, STORE)):
            nc.sync.dma_start(hidden_sb[:, half], hidden[:, half])
        offsets = held.tile([P, N // 16], U16, name="offsets")
        nc.sync.dma_start(offsets[:], offs)
        wq_sb = held.tile([P, P], BF16)
        nc.sync.dma_start(wq_sb[:], wq)
        bq_sb = held.tile([P, 1], F32)
        beta_sb = held.tile([P, 1], F32)
        mem_z = held.tile([P, P + 1], BF16)
        with nc.allow_non_contiguous_dma(reason="one element to a partition"):
            nc.sync.dma_start(bq_sb[:], bq)
            nc.sync.dma_start(beta_sb[:], beta.partition_broadcast(P))
            nc.sync.dma_start(mem_z[:, 0:P], mem)
            nc.sync.dma_start(mem_z[:, P : P + 1], z)
        ident = held.tile([P, P], F32)
        nc.vector.memset(ident[:], 0.0)
        make_identity(nc, ident[:], nomemset=True)

        zero = held.tile([P, 1], F32)
        nc.vector.memset(zero[:], 0.0)
        exp_zero = held.tile([P, 1], F32)
        nc.scalar.activation(exp_zero[:], zero[:], ACT.Exp)

        bq_plus1 = held.tile([P, 1], F32)
        nc.vector.tensor_scalar_add(bq_plus1[:], bq_sb[:], 1.0)
        half_bq = held.tile([P, 1], F32)
        nc.vector.tensor_scalar_mul(half_bq[:], bq_sb[:], 0.5)
        minus_half_bq = held.tile([P, 1], F32)
        nc.vector.tensor_scalar_mul(minus_half_bq[:], bq_sb[:], -0.5)
        tanh_half = held.tile([P, 1], F32)
        nc.scalar.activation(tanh_half[:], beta_sb[:], ACT.Tanh, scale=0.5)
        rest = held.tile([P, 1], F32)
        nc.vector.tensor_scalar(rest[:], tanh_half[:], -0.5, 0.5, op0=ALU.mult, op1=ALU.add)
        rest_bq = held.tile([P, 1], F32)
        nc.vector.tensor_scalar(rest_bq[:], tanh_half[:], minus_half_bq[:], half_bq[:], op0=ALU.mult, op1=ALU.add)
        mix = held.tile([P, 1], F32)
        nc.vector.tensor_scalar(mix[:], tanh_half[:], 0.5, 0.5, op0=ALU.mult, op1=ALU.add)

        q_ps = []
        for start, width in zip(STEP_STARTS, STEP_WIDTHS):
            q_step = banks.tile([P, BANK], F32, tag="bank")
            picked = hidden_sb[:].indirect(offsets[:, start // 16 : (start + width) // 16])
            nc.tensor.matmul(q_step[:, 0:width], wq_sb[:], picked, start=True, stop=True)
            q_ps.append(q_step)

        sq = []
        num_den_ps = []
        inv_dens = []
        read_t = []
        for t in range(STEPS + 2 * LAG):
            if t < STEPS:
                width = STEP_WIDTHS[t]
                exp_q = work.tile([P, width], BF16, tag="exp_q")
                nc.scalar.activation(exp_q[:], q_ps[t][:, 0:width], ACT.Exp, bias=bq_sb[:])
                exp_cut = work.tile([P, width], BF16, tag="exp_cut")
                nc.vector.tensor_scalar_min(exp_cut[:], exp_q[:], 1.0)
                sq_step = work.tile([P, width], BF16, tag="sq_step")
                nc.vector.scalar_tensor_tensor(
                    sq_step[:], q_ps[t][:, 0:width], bq_plus1[:], exp_cut[:], op0=ALU.add, op1=ALU.max
                )
                sq.append(sq_step)
            s = t - LAG
            if 0 <= s < STEPS:
                blocks = STEP_WIDTHS[s] // BLOCK
                num_den = banks.tile([P, MAX_BLOCKS, BANK // MAX_BLOCKS], F32, tag="bank")
                for b in range(blocks):
                    nc.tensor.matmul(
                        num_den[:, b, 0 : P + 1], sq[s][:, b * BLOCK : (b + 1) * BLOCK], mem_z[:], start=True, stop=True
                    )
                inv_den = work.tile([P, MAX_BLOCKS, 1], F32)
                nc.vector.reciprocal(inv_den[:, 0:blocks, :], num_den[:, 0:blocks, P : P + 1])
                num_den_ps.append(num_den)
                inv_dens.append(inv_den)
            s = t - 2 * LAG
            if s >= 0:
                r = work.tile([P, MAX_BLOCKS, BLOCK], F32)
                for b in range(STEP_WIDTHS[s] // BLOCK):
                    num, factor = num_den_ps[s][:, b, 0:P], inv_dens[s][:, b, :]
                    if s < STEPS // 2:
                        nc.vector.tensor_scalar_mul(r[:, b, :], num, factor)
                    else:
                        nc.scalar.activation(r[:, b, :], num, ACT.Identity, scale=factor)
                read_t.append(r)

        q_share = []
        for s in range(STEPS):
            width = STEP_WIDTHS[s]
            share_step = work.tile([P, width], F32, tag="share_step")
            nc.scalar.activation(share_step[:], q_ps[s][:, 0:width], ACT.Identity, bias=rest_bq[:], scale=rest[:])
            q_share.append(share_step)

        for s in range(STEPS):
            start, width = STEP_STARTS[s], STEP_WIDTHS[s]
            read_ps = banks.tile([P, BANK], F32, tag="bank")
            for b in range(width // BLOCK):
                nc.tensor.transpose(read_ps[:, b * BLOCK : (b + 1) * BLOCK], read_t[s][:, b, :], ident[:])
            out_sb = work.tile([P, width], F32, tag="out_sb")
            nc.vector.scalar_tensor_tensor(
                out_sb[:], read_ps[:, 0:width], mix[:], q_share[s][:], op0=ALU.mult, op1=ALU.add
            )
            nc.sync.dma_start(out[:, start : start + width], out_sb[:])
